import numpy as np
import ml_dtypes


def mxq(x, axis, fmt="e4m3"):
    dtype, down = {"e4m3": (ml_dtypes.float8_e4m3fn, 7), "e5m2": (ml_dtypes.float8_e5m2, 14)}[fmt]
    v = np.moveaxis(np.asarray(x, np.float32).astype(ml_dtypes.bfloat16).astype(np.float64), axis, -1)
    blocks = v.reshape(v.shape[:-1] + (-1, 32))
    amax = np.abs(blocks).max(-1, keepdims=True)
    byte = np.maximum(np.where(amax > 0, np.frexp(amax)[1] - 1 + 127, 0) - down, 1)
    scale = np.exp2(byte - 127.0)
    codes = (blocks / scale).astype(np.float32).astype(dtype).astype(np.float64)
    return np.moveaxis((codes * scale).reshape(v.shape), -1, axis)


WIDE = False


def mx_kscale(k):
    if not WIDE:
        return np.ones(k)
    levels = np.array([10, -10, 5, -5, 0])
    if k % 512:
        return np.exp2(np.random.permutation(np.resize(levels, k // 32))).repeat(32)
    a = np.empty((k // 512, 16))
    for p in range(k // 512):
        a[p, :8] = np.random.permutation(np.resize(levels, 8))
        for g in range(8):
            far = levels[np.abs(levels - a[p, g]) >= 10]
            a[p, g + 8] = far[np.random.randint(len(far))]
    return np.exp2(a.ravel()).repeat(32)


BF16 = ml_dtypes.bfloat16


def bf(x):
    return np.asarray(x, np.float32).astype(BF16)


def f64(x):
    return np.asarray(x).astype(np.float64)


NB, D, CO, CV, R = 16, 256, 128, 512, 512


def setup_inputs():
    s, t = mx_kscale(CV), mx_kscale(R)
    return {"x1": bf(np.random.standard_normal((NB, D, CO))),
            "A": bf(np.random.standard_normal((D, R)) / np.sqrt(D) * t),
            "t2": bf(np.random.standard_normal((NB, R, CV)) * s),
            "w": bf(np.random.standard_normal((NB, CO, CV)) / np.sqrt(CV) / s),
            "C": bf(np.random.standard_normal((D, R)) / np.sqrt(R) / t)}


def reference(x1, A, t2, w, C):
    t1 = f64(A).T @ f64(x1)
    t3 = mxq(f64(t2), 2, "e4m3") @ mxq(f64(w).transpose(0, 2, 1), 1, "e4m3")
    h = t1 * t3
    return mxq(f64(C), 1, "e4m3") @ mxq(h, 1, "e4m3")

@@ -1,0 +1,279 @@
+from contextlib import ExitStack
+
+import concourse.mybir as mybir
+from concourse.masks import make_identity
+
+F32 = mybir.dt.float32
+BF16 = mybir.dt.bfloat16
+U32 = mybir.dt.uint32
+U8 = mybir.dt.uint8
+FP8X4 = mybir.dt.float8_e4m3fn_x4
+
+NB, D, CO, CV, R = 16, 256, 128, 512, 512
+P = 128
+PACK = 4
+HALVES = 2
+D_ROWS = D // P
+RUN = 2
+GROUP = 4
+PSUM_BANKS = 8
+
+FLOPS = 2 * NB * R * CO * (D + CV) + 2 * NB * D * CO * R
+
+AT_PROJECT = 0
+AT_TRANSPOSE = 3
+AT_QUANTISE = 4
+AT_T3 = 5
+AT_MULTIPLY = 6
+AT_QUANTISE_H = 7
+AT_OUT = 8
+ROUND_OF_C = 5
+
+
+def tile_cptensorproduct_pa_kernel(tc, x1, A, t2, w, C, out):
+    nc = tc.nc
+    with ExitStack() as ctx:
+        consts = ctx.enter_context(tc.tile_pool(name="consts", bufs=1))
+        x1_pool = ctx.enter_context(tc.tile_pool(name="x1_pool", bufs=NB // GROUP))
+        w_pool = ctx.enter_context(tc.tile_pool(name="w_pool", bufs=NB // GROUP))
+        t2_pool = ctx.enter_context(tc.tile_pool(name="t2_pool", bufs=NB))
+        work = ctx.enter_context(tc.tile_pool(name="work", bufs=4))
+        t1_pool = ctx.enter_context(tc.tile_pool(name="t1_pool", bufs=AT_MULTIPLY - AT_PROJECT + 2))
+        out_pool = ctx.enter_context(tc.tile_pool(name="out_pool", bufs=NB))
+        psum = ctx.enter_context(tc.psum_pool(name="psum", bufs=PSUM_BANKS))
+
+        ctx.enter_context(tc.manual_schedule())
+
+        def is_sample(b):
+            return 0 <= b < NB
+
+        def opens_run(b):
+            return is_sample(b) and b % RUN == 0
+
+        def opens_group(b):
+            return is_sample(b) and b % GROUP == 0
+
+        x1_tiles = []
+        w_tiles = []
+        t2_tiles = []
+        w_rows = w.rearrange("b o v -> (b o) v")
+
+        a_in = consts.tile([P, D_ROWS * R], BF16)
+        nc.sync.dma_start(out=a_in[:], in_=A.rearrange("(p i) r -> p (i r)", i=D_ROWS))
+        c_in = consts.tile([P, D_ROWS * R], BF16)
+        for n in range(NB + AT_TRANSPOSE):
+            if opens_group(n - AT_PROJECT):
+                b = n - AT_PROJECT
+                x1_in = x1_pool.tile([P, GROUP, D_ROWS * CO], BF16)
+                nc.sync.dma_start(
+                    out=x1_in[:],
+                    in_=x1[b : b + GROUP].rearrange("b (p i) c -> p b (i c)", i=D_ROWS),
+                )
+                x1_tiles.append(x1_in)
+            if n == ROUND_OF_C:
+                nc.sync.dma_start(out=c_in[:], in_=C.rearrange("(p i) r -> p (i r)", i=D_ROWS))
+            if opens_group(n - AT_TRANSPOSE):
+                b = n - AT_TRANSPOSE
+                w_in = w_pool.tile([P, PACK * CV], BF16)
+                nc.sync.dma_start(
+                    out=w_in[:],
+                    in_=w_rows[b * CO : (b + GROUP) * CO].rearrange("(p i) v -> p (i v)", i=PACK),
+                )
+                w_tiles.append(w_in)
+            if opens_run(n - AT_TRANSPOSE):
+                for b in range(n - AT_TRANSPOSE, n - AT_TRANSPOSE + RUN):
+                    t2_in = t2_pool.tile([P, PACK * CV], BF16)
+                    nc.sync.dma_start(out=t2_in[:], in_=t2[b].rearrange("(p j) v -> p (j v)", j=PACK))
+                    t2_tiles.append(t2_in)
+
+        ident = consts.tile([P, P], F32)
+        make_identity(nc, ident[:])
+
+        a_chunks = consts.tile([P, D_ROWS, PACK, P], BF16)
+        nc.vector.tensor_copy(
+            out=a_chunks[:],
+            in_=a_in[:].rearrange("p (i m j) -> p i j m", i=D_ROWS, j=PACK),
+        )
+
+        c_grouped = consts.tile([P, D_ROWS * P * PACK], BF16, align_bytes=64)
+        c_codes = consts.tile([P, D_ROWS * P], U32, align_bytes=64)
+        c_scales = consts.tile([P, D_ROWS * P], U8, align_bytes=64)
+
+        t1_tiles = {}
+        t2_grouped_tiles = {}
+        w_grouped_tiles = {}
+        t2_mx = {}
+        w_mx = {}
+        t3_tiles = {}
+        h_grouped_tiles = {}
+        h_mx = {}
+
+        def transpose_c():
+            c_words = c_in[:].bitcast(F32)
+            cT_ps = psum.tile([P, D_ROWS, HALVES, P], F32, tag="bank")
+            for i in range(D_ROWS):
+                for u in range(HALVES):
+                    nc.tensor.transpose(
+                        cT_ps[:, i, u, :],
+                        c_words[:, i * (R // 2) + u : (i + 1) * (R // 2) : 2],
+                        ident[:],
+                    )
+            nc.vector.tensor_copy(
+                out=c_grouped[:].bitcast(F32).rearrange("p (i d u) -> p i d u", i=D_ROWS, u=HALVES),
+                in_=cT_ps[:].rearrange("p i u d -> p i d u"),
+            )
+
+        def quantise_c():
+            nc.vector.quantize_mx(out=c_codes[:].bitcast(FP8X4), scales=c_scales[:], in_=c_grouped[:])
+
+        def project(b):
+            x1_b = x1_tiles[b // GROUP][:, b % GROUP, :]
+            t1_ps = psum.tile([P, PACK, CO], F32, tag="bank")
+            for j in range(PACK):
+                for i in range(D_ROWS):
+                    nc.tensor.matmul(
+                        out=t1_ps[:, j, :],
+                        lhsT=a_chunks[:, i, j, :],
+                        rhs=x1_b[:, i * CO : (i + 1) * CO],
+                        start=(i == 0),
+                        stop=(i == D_ROWS - 1),
+                    )
+            t1_sb = t1_pool.tile([P, CO, PACK], F32)
+            nc.scalar.copy(out=t1_sb[:], in_=t1_ps[:].rearrange("p j c -> p c j"))
+            t1_tiles[b] = t1_sb
+
+        def transpose_w(g):
+            w_words = w_tiles[g][:].bitcast(F32)
+            w_grouped = work.tile([P, GROUP * CO * PACK], BF16, align_bytes=64)
+            grouped_words = w_grouped[:].bitcast(F32).rearrange("p (q i u) -> p q i u", i=PACK, u=HALVES)
+            for k in range(PACK // 2):
+                wT_ps = psum.tile([P, 2, HALVES, P], F32, tag="bank")
+                for ii in range(2):
+                    for u in range(HALVES):
+                        row = (2 * k + ii) * (CV // 2)
+                        nc.tensor.transpose(
+                            wT_ps[:, ii, u, :], w_words[:, row + u : row + CV // 2 : HALVES], ident[:]
+                        )
+                nc.vector.tensor_copy(
+                    out=grouped_words[:, :, 2 * k : 2 * k + 2, :],
+                    in_=wT_ps[:].rearrange("p ii u q -> p q ii u"),
+                )
+            w_grouped_tiles[g] = w_grouped
+
+        def transpose_t2(b):
+            t2_words = t2_tiles[b][:].bitcast(F32)
+            t2_grouped = work.tile([P, PACK * P * PACK], BF16, align_bytes=64)
+            grouped_words = t2_grouped[:].bitcast(F32).rearrange("p (j m u) -> p j m u", j=PACK, u=HALVES)
+            for k in range(PACK // 2):
+                t2T_ps = psum.tile([P, 2, HALVES, P], F32, tag="bank")
+                for jj in range(2):
+                    for u in range(HALVES):
+                        row = (2 * k + jj) * (CV // 2)
+                        nc.tensor.transpose(
+                            t2T_ps[:, jj, u, :], t2_words[:, row + u : row + CV // 2 : HALVES], ident[:]
+                        )
+                nc.scalar.copy(
+                    out=grouped_words[:, 2 * k : 2 * k + 2],
+                    in_=t2T_ps[:].rearrange("p jj u m -> p jj m u"),
+                )
+            t2_grouped_tiles[b] = t2_grouped
+
+        def quantise_t2(b):
+            t2_codes = work.tile([P, PACK * P], U32, align_bytes=64)
+            t2_scales = work.tile([P, PACK * P], U8, align_bytes=64)
+            nc.vector.quantize_mx(
+                out=t2_codes[:].bitcast(FP8X4), scales=t2_scales[:], in_=t2_grouped_tiles[b][:]
+            )
+            t2_mx[b] = (t2_codes, t2_scales)
+
+        def quantise_w(g):
+            w_codes = work.tile([P, GROUP * CO], U32, align_bytes=64)
+            w_scales = work.tile([P, GROUP * CO], U8, align_bytes=64)
+            nc.vector.quantize_mx(
+                out=w_codes[:].bitcast(FP8X4), scales=w_scales[:], in_=w_grouped_tiles[g][:]
+            )
+            w_mx[g] = (w_codes, w_scales)
+
+        def contract_channels(b):
+            t2_codes, t2_scales = t2_mx[b]
+            w_codes, w_scales = w_mx[b // GROUP]
+            w_cols = slice((b % GROUP) * CO, (b % GROUP + 1) * CO)
+            t3_ps = psum.tile([P, PACK, CO], F32, tag="bank")
+            for j in range(PACK):
+                ranks = slice(j * P, (j + 1) * P)
+                nc.tensor.matmul_mx(
+                    out=t3_ps[:, j, :],
+                    lhsT=t2_codes[:, ranks].bitcast(FP8X4),
+                    lhsT_scale=t2_scales[:, ranks],
+                    rhs=w_codes[:, w_cols].bitcast(FP8X4),
+                    rhs_scale=w_scales[:, w_cols],
+                    start=True,
+                    stop=True,
+                )
+            t3_tiles[b] = t3_ps
+
+        def multiply(b):
+            h_grouped = work.tile([P, CO, PACK], BF16, align_bytes=64)
+            nc.vector.tensor_tensor(
+                out=h_grouped[:],
+                in0=t1_tiles[b][:],
+                in1=t3_tiles[b][:].rearrange("p j c -> p c j"),
+                op=mybir.AluOpType.mult,
+            )
+            h_grouped_tiles[b] = h_grouped
+
+        def quantise_h(b):
+            h_codes = work.tile([P, CO], U32, align_bytes=64)
+            h_scales = work.tile([P, CO], U8, align_bytes=64)
+            nc.vector.quantize_mx(
+                out=h_codes[:].bitcast(FP8X4),
+                scales=h_scales[:],
+                in_=h_grouped_tiles[b][:].rearrange("p c t -> p (c t)"),
+            )
+            h_mx[b] = (h_codes, h_scales)
+
+        def contract_ranks(b):
+            h_codes, h_scales = h_mx[b]
+            out_ps = psum.tile([P, D_ROWS, CO], F32, tag="bank")
+            for i in range(D_ROWS):
+                comps = slice(i * P, (i + 1) * P)
+                nc.tensor.matmul_mx(
+                    out=out_ps[:, i, :],
+                    lhsT=c_codes[:, comps].bitcast(FP8X4),
+                    lhsT_scale=c_scales[:, comps],
+                    rhs=h_codes[:].bitcast(FP8X4),
+                    rhs_scale=h_scales[:],
+                    start=True,
+                    stop=True,
+                )
+            out_sb = out_pool.tile([P, D_ROWS, CO], F32)
+            nc.scalar.copy(out=out_sb[:], in_=out_ps[:])
+            nc.sync.dma_start(
+                out=out[b].rearrange("(p i) c -> p (i c)", i=D_ROWS),
+                in_=out_sb[:].rearrange("p i c -> p (i c)"),
+            )
+
+        for n in range(NB + AT_OUT):
+            if is_sample(n - AT_QUANTISE):
+                quantise_t2(n - AT_QUANTISE)
+            if opens_group(n - AT_QUANTISE):
+                quantise_w((n - AT_QUANTISE) // GROUP)
+            if n == ROUND_OF_C + 1:
+                quantise_c()
+            if is_sample(n - AT_MULTIPLY):
+                multiply(n - AT_MULTIPLY)
+            if is_sample(n - AT_QUANTISE_H):
+                quantise_h(n - AT_QUANTISE_H)
+            if n == ROUND_OF_C:
+                transpose_c()
+            if opens_group(n - AT_TRANSPOSE):
+                transpose_w((n - AT_TRANSPOSE) // GROUP)
+            if opens_run(n - AT_TRANSPOSE):
+                for b in range(n - AT_TRANSPOSE, n - AT_TRANSPOSE + RUN):
+                    transpose_t2(b)
+            if is_sample(n - AT_PROJECT):
+                project(n - AT_PROJECT)
+            if is_sample(n - AT_T3):
+                contract_channels(n - AT_T3)
+            if is_sample(n - AT_OUT):
+                contract_ranks(n - AT_OUT)

@@ -14,77 +14,65 @@ P = 128
 PACK = 4
 HALVES = 2
 D_ROWS = D // P
-RUN = 2
-GROUP = 4
-PSUM_BANKS = 8
+PAIR = 2
+W_ROWS = PAIR * CO // P
+PAIRS = NB // PAIR
+WORDS = CV // 2
 
 FLOPS = 2 * NB * R * CO * (D + CV) + 2 * NB * D * CO * R
-
-AT_PROJECT = 0
-AT_TRANSPOSE = 3
-AT_QUANTISE = 4
-AT_T3 = 5
-AT_MULTIPLY = 6
-AT_QUANTISE_H = 7
-AT_OUT = 8
-ROUND_OF_C = 5
 
 
 def tile_cptensorproduct_pa_kernel(tc, x1, A, t2, w, C, out):
     nc = tc.nc
     with ExitStack() as ctx:
         consts = ctx.enter_context(tc.tile_pool(name="consts", bufs=1))
-        x1_pool = ctx.enter_context(tc.tile_pool(name="x1_pool", bufs=NB // GROUP))
-        w_pool = ctx.enter_context(tc.tile_pool(name="w_pool", bufs=NB // GROUP))
+        loads = ctx.enter_context(tc.tile_pool(name="loads", bufs=PAIRS))
         t2_pool = ctx.enter_context(tc.tile_pool(name="t2_pool", bufs=NB))
         work = ctx.enter_context(tc.tile_pool(name="work", bufs=4))
-        t1_pool = ctx.enter_context(tc.tile_pool(name="t1_pool", bufs=AT_MULTIPLY - AT_PROJECT + 2))
-        out_pool = ctx.enter_context(tc.tile_pool(name="out_pool", bufs=NB))
-        psum = ctx.enter_context(tc.psum_pool(name="psum", bufs=PSUM_BANKS))
+        t1_pool = ctx.enter_context(tc.tile_pool(name="t1_pool", bufs=5))
+        out_pool = ctx.enter_context(tc.tile_pool(name="out_pool", bufs=PAIRS + 1))
+        psum = ctx.enter_context(tc.psum_pool(name="psum", bufs=8))
 
         ctx.enter_context(tc.manual_schedule())
-
-        def is_sample(b):
-            return 0 <= b < NB
-
-        def opens_run(b):
-            return is_sample(b) and b % RUN == 0
-
-        def opens_group(b):
-            return is_sample(b) and b % GROUP == 0
 
         x1_tiles = []
         w_tiles = []
         t2_tiles = []
         w_rows = w.rearrange("b o v -> (b o) v")
 
+        def load_x1(k):
+            x1_in = loads.tile([P, PAIR, D_ROWS * CO], BF16)
+            nc.sync.dma_start(
+                out=x1_in[:],
+                in_=x1[k * PAIR : (k + 1) * PAIR].rearrange("b (p i) c -> p b (i c)", i=D_ROWS),
+            )
+            x1_tiles.append(x1_in)
+
+        def load_w(k):
+            w_in = loads.tile([P, W_ROWS * CV], BF16)
+            nc.sync.dma_start(
+                out=w_in[:],
+                in_=w_rows[k * PAIR * CO : (k + 1) * PAIR * CO].rearrange("(p i) v -> p (i v)", i=W_ROWS),
+            )
+            w_tiles.append(w_in)
+
+        def load_t2(b):
+            t2_in = t2_pool.tile([P, PACK * CV], BF16)
+            nc.sync.dma_start(out=t2_in[:], in_=t2[b].rearrange("(p j) v -> p (j v)", j=PACK))
+            t2_tiles.append(t2_in)
+
         a_in = consts.tile([P, D_ROWS * R], BF16)
         nc.sync.dma_start(out=a_in[:], in_=A.rearrange("(p i) r -> p (i r)", i=D_ROWS))
         c_in = consts.tile([P, D_ROWS * R], BF16)
-        for n in range(NB + AT_TRANSPOSE):
-            if opens_group(n - AT_PROJECT):
-                b = n - AT_PROJECT
-                x1_in = x1_pool.tile([P, GROUP, D_ROWS * CO], BF16)
-                nc.sync.dma_start(
-                    out=x1_in[:],
-                    in_=x1[b : b + GROUP].rearrange("b (p i) c -> p b (i c)", i=D_ROWS),
-                )
-                x1_tiles.append(x1_in)
-            if n == ROUND_OF_C:
+        load_x1(0)
+        for k in range(PAIRS):
+            load_w(k)
+            load_t2(k * PAIR)
+            if k + 1 < PAIRS:
+                load_x1(k + 1)
+            load_t2(k * PAIR + 1)
+            if k == 0:
                 nc.sync.dma_start(out=c_in[:], in_=C.rearrange("(p i) r -> p (i r)", i=D_ROWS))
-            if opens_group(n - AT_TRANSPOSE):
-                b = n - AT_TRANSPOSE
-                w_in = w_pool.tile([P, PACK * CV], BF16)
-                nc.sync.dma_start(
-                    out=w_in[:],
-                    in_=w_rows[b * CO : (b + GROUP) * CO].rearrange("(p i) v -> p (i v)", i=PACK),
-                )
-                w_tiles.append(w_in)
-            if opens_run(n - AT_TRANSPOSE):
-                for b in range(n - AT_TRANSPOSE, n - AT_TRANSPOSE + RUN):
-                    t2_in = t2_pool.tile([P, PACK * CV], BF16)
-                    nc.sync.dma_start(out=t2_in[:], in_=t2[b].rearrange("(p j) v -> p (j v)", j=PACK))
-                    t2_tiles.append(t2_in)
 
         ident = consts.tile([P, P], F32)
         make_identity(nc, ident[:])
@@ -99,105 +87,106 @@ def tile_cptensorproduct_pa_kernel(tc, x1, A, t2, w, C, out):
         c_codes = consts.tile([P, D_ROWS * P], U32, align_bytes=64)
         c_scales = consts.tile([P, D_ROWS * P], U8, align_bytes=64)
 
+        t1_ps = {}
         t1_tiles = {}
-        t2_grouped_tiles = {}
-        w_grouped_tiles = {}
-        t2_mx = {}
+        w_ps = {}
+        w_grouped = {}
         w_mx = {}
+        t2_ps = {}
+        t2_grouped = {}
+        t2_mx = {}
+        c_ps = {}
         t3_tiles = {}
-        h_grouped_tiles = {}
+        h_tiles = {}
         h_mx = {}
 
-        def transpose_c():
-            c_words = c_in[:].bitcast(F32)
-            cT_ps = psum.tile([P, D_ROWS, HALVES, P], F32, tag="bank")
-            for i in range(D_ROWS):
-                for u in range(HALVES):
-                    nc.tensor.transpose(
-                        cT_ps[:, i, u, :],
-                        c_words[:, i * (R // 2) + u : (i + 1) * (R // 2) : 2],
-                        ident[:],
-                    )
-            nc.vector.tensor_copy(
-                out=c_grouped[:].bitcast(F32).rearrange("p (i d u) -> p i d u", i=D_ROWS, u=HALVES),
-                in_=cT_ps[:].rearrange("p i u d -> p i d u"),
+
+        def project(k, a, j, i):
+            if (j, i) == (0, 0):
+                bank = psum.tile([P, 2, PAIR, CO], F32, tag="bank")
+                t1_ps[k, a] = bank
+                if a == 0:
+                    t1_sb = t1_pool.tile([P, PACK // 2, PAIR, CO, 2], F32)
+                    t1_tiles[k] = t1_sb
+            nc.tensor.matmul(
+                out=t1_ps[k, a][:, j],
+                lhsT=a_chunks[:, i, 2 * a + j, :],
+                rhs=x1_tiles[k][:, :, i * CO : (i + 1) * CO],
+                start=(i == 0),
+                stop=(i == D_ROWS - 1),
             )
+            if (j, i) == (1, D_ROWS - 1):
+                nc.scalar.copy(out=t1_tiles[k][:, a], in_=t1_ps[k, a][:].rearrange("p j b c -> p b c j"))
+
+        def transpose_w(k, i, u):
+            if (i, u) == (0, 0):
+                bank = psum.tile([P, W_ROWS, HALVES, P], F32, tag="bank")
+                w_ps[k] = bank
+            words = w_tiles[k][:].bitcast(F32)
+            nc.tensor.transpose(
+                w_ps[k][:, i, u, :], words[:, i * WORDS + u : (i + 1) * WORDS : HALVES], ident[:]
+            )
+            if (i, u) == (W_ROWS - 1, HALVES - 1):
+                grouped = work.tile([P, PAIR * CO * PACK], BF16, align_bytes=64)
+                nc.vector.tensor_copy(
+                    out=grouped[:].bitcast(F32).rearrange("p (q i u) -> p q i u", i=W_ROWS, u=HALVES),
+                    in_=w_ps[k][:].rearrange("p i u q -> p q i u"),
+                )
+                w_grouped[k] = grouped
+
+        def transpose_t2(b, m, j, u):
+            if (j, u) == (0, 0):
+                bank = psum.tile([P, 2, HALVES, P], F32, tag="bank")
+                t2_ps[b, m] = bank
+                if m == 0:
+                    grouped = work.tile([P, PACK * P * PACK], BF16, align_bytes=64)
+                    t2_grouped[b] = grouped
+            words = t2_tiles[b][:].bitcast(F32)
+            row = (2 * m + j) * WORDS
+            nc.tensor.transpose(
+                t2_ps[b, m][:, j, u, :], words[:, row + u : row + WORDS : HALVES], ident[:]
+            )
+            if (j, u) == (1, HALVES - 1):
+                out_words = t2_grouped[b][:].bitcast(F32).rearrange("p (j r u) -> p j r u", j=PACK, u=HALVES)
+                nc.scalar.copy(
+                    out=out_words[:, 2 * m : 2 * m + 2],
+                    in_=t2_ps[b, m][:].rearrange("p j u r -> p j r u"),
+                )
+
+        def transpose_c(i, u):
+            if (i, u) == (0, 0):
+                bank = psum.tile([P, D_ROWS, HALVES, P], F32, tag="bank")
+                c_ps[0] = bank
+            words = c_in[:].bitcast(F32)
+            nc.tensor.transpose(
+                c_ps[0][:, i, u, :], words[:, i * (R // 2) + u : (i + 1) * (R // 2) : HALVES], ident[:]
+            )
+            if (i, u) == (D_ROWS - 1, HALVES - 1):
+                nc.vector.tensor_copy(
+                    out=c_grouped[:].bitcast(F32).rearrange("p (i d u) -> p i d u", i=D_ROWS, u=HALVES),
+                    in_=c_ps[0][:].rearrange("p i u d -> p i d u"),
+                )
+
+
+        def quantise_w(k):
+            codes = work.tile([P, PAIR * CO], U32, align_bytes=64)
+            scales = work.tile([P, PAIR * CO], U8, align_bytes=64)
+            nc.vector.quantize_mx(out=codes[:].bitcast(FP8X4), scales=scales[:], in_=w_grouped[k][:])
+            w_mx[k] = (codes, scales)
+
+        def quantise_t2(b):
+            codes = work.tile([P, PACK * P], U32, align_bytes=64)
+            scales = work.tile([P, PACK * P], U8, align_bytes=64)
+            nc.vector.quantize_mx(out=codes[:].bitcast(FP8X4), scales=scales[:], in_=t2_grouped[b][:])
+            t2_mx[b] = (codes, scales)
 
         def quantise_c():
             nc.vector.quantize_mx(out=c_codes[:].bitcast(FP8X4), scales=c_scales[:], in_=c_grouped[:])
 
-        def project(b):
-            x1_b = x1_tiles[b // GROUP][:, b % GROUP, :]
-            t1_ps = psum.tile([P, PACK, CO], F32, tag="bank")
-            for j in range(PACK):
-                for i in range(D_ROWS):
-                    nc.tensor.matmul(
-                        out=t1_ps[:, j, :],
-                        lhsT=a_chunks[:, i, j, :],
-                        rhs=x1_b[:, i * CO : (i + 1) * CO],
-                        start=(i == 0),
-                        stop=(i == D_ROWS - 1),
-                    )
-            t1_sb = t1_pool.tile([P, CO, PACK], F32)
-            nc.scalar.copy(out=t1_sb[:], in_=t1_ps[:].rearrange("p j c -> p c j"))
-            t1_tiles[b] = t1_sb
-
-        def transpose_w(g):
-            w_words = w_tiles[g][:].bitcast(F32)
-            w_grouped = work.tile([P, GROUP * CO * PACK], BF16, align_bytes=64)
-            grouped_words = w_grouped[:].bitcast(F32).rearrange("p (q i u) -> p q i u", i=PACK, u=HALVES)
-            for k in range(PACK // 2):
-                wT_ps = psum.tile([P, 2, HALVES, P], F32, tag="bank")
-                for ii in range(2):
-                    for u in range(HALVES):
-                        row = (2 * k + ii) * (CV // 2)
-                        nc.tensor.transpose(
-                            wT_ps[:, ii, u, :], w_words[:, row + u : row + CV // 2 : HALVES], ident[:]
-                        )
-                nc.vector.tensor_copy(
-                    out=grouped_words[:, :, 2 * k : 2 * k + 2, :],
-                    in_=wT_ps[:].rearrange("p ii u q -> p q ii u"),
-                )
-            w_grouped_tiles[g] = w_grouped
-
-        def transpose_t2(b):
-            t2_words = t2_tiles[b][:].bitcast(F32)
-            t2_grouped = work.tile([P, PACK * P * PACK], BF16, align_bytes=64)
-            grouped_words = t2_grouped[:].bitcast(F32).rearrange("p (j m u) -> p j m u", j=PACK, u=HALVES)
-            for k in range(PACK // 2):
-                t2T_ps = psum.tile([P, 2, HALVES, P], F32, tag="bank")
-                for jj in range(2):
-                    for u in range(HALVES):
-                        row = (2 * k + jj) * (CV // 2)
-                        nc.tensor.transpose(
-                            t2T_ps[:, jj, u, :], t2_words[:, row + u : row + CV // 2 : HALVES], ident[:]
-                        )
-                nc.scalar.copy(
-                    out=grouped_words[:, 2 * k : 2 * k + 2],
-                    in_=t2T_ps[:].rearrange("p jj u m -> p jj m u"),
-                )
-            t2_grouped_tiles[b] = t2_grouped
-
-        def quantise_t2(b):
-            t2_codes = work.tile([P, PACK * P], U32, align_bytes=64)
-            t2_scales = work.tile([P, PACK * P], U8, align_bytes=64)
-            nc.vector.quantize_mx(
-                out=t2_codes[:].bitcast(FP8X4), scales=t2_scales[:], in_=t2_grouped_tiles[b][:]
-            )
-            t2_mx[b] = (t2_codes, t2_scales)
-
-        def quantise_w(g):
-            w_codes = work.tile([P, GROUP * CO], U32, align_bytes=64)
-            w_scales = work.tile([P, GROUP * CO], U8, align_bytes=64)
-            nc.vector.quantize_mx(
-                out=w_codes[:].bitcast(FP8X4), scales=w_scales[:], in_=w_grouped_tiles[g][:]
-            )
-            w_mx[g] = (w_codes, w_scales)
-
         def contract_channels(b):
             t2_codes, t2_scales = t2_mx[b]
-            w_codes, w_scales = w_mx[b // GROUP]
-            w_cols = slice((b % GROUP) * CO, (b % GROUP + 1) * CO)
+            w_codes, w_scales = w_mx[b // PAIR]
+            w_cols = slice((b % PAIR) * CO, (b % PAIR + 1) * CO)
             t3_ps = psum.tile([P, PACK, CO], F32, tag="bank")
             for j in range(PACK):
                 ranks = slice(j * P, (j + 1) * P)
@@ -213,67 +202,112 @@ def tile_cptensorproduct_pa_kernel(tc, x1, A, t2, w, C, out):
             t3_tiles[b] = t3_ps
 
         def multiply(b):
-            h_grouped = work.tile([P, CO, PACK], BF16, align_bytes=64)
+            k, s = divmod(b, PAIR)
+            if s == 0:
+                h_pair = work.tile([P, PAIR, CO, PACK], BF16, align_bytes=64)
+                h_tiles[k] = h_pair
             nc.vector.tensor_tensor(
-                out=h_grouped[:],
-                in0=t1_tiles[b][:],
-                in1=t3_tiles[b][:].rearrange("p j c -> p c j"),
+                out=h_tiles[k][:, s].rearrange("p c (a j) -> p c a j", a=PACK // 2),
+                in0=t1_tiles[k][:, :, s].rearrange("p a c j -> p c a j"),
+                in1=t3_tiles[b][:].rearrange("p (a j) c -> p c a j", a=PACK // 2),
                 op=mybir.AluOpType.mult,
             )
-            h_grouped_tiles[b] = h_grouped
 
-        def quantise_h(b):
-            h_codes = work.tile([P, CO], U32, align_bytes=64)
-            h_scales = work.tile([P, CO], U8, align_bytes=64)
+        def quantise_h(b, count):
+            k, s = divmod(b, PAIR)
+            codes = work.tile([P, PAIR * CO], U32, align_bytes=64)
+            scales = work.tile([P, PAIR * CO], U8, align_bytes=64)
             nc.vector.quantize_mx(
-                out=h_codes[:].bitcast(FP8X4),
-                scales=h_scales[:],
-                in_=h_grouped_tiles[b][:].rearrange("p c t -> p (c t)"),
+                out=codes[:, : count * CO].bitcast(FP8X4),
+                scales=scales[:, : count * CO],
+                in_=h_tiles[k][:, s : s + count].rearrange("p b c t -> p (b c t)"),
             )
-            h_mx[b] = (h_codes, h_scales)
+            h_mx[b] = (codes, scales)
 
-        def contract_ranks(b):
-            h_codes, h_scales = h_mx[b]
-            out_ps = psum.tile([P, D_ROWS, CO], F32, tag="bank")
+        def contract_ranks(b, count):
+            codes, scales = h_mx[b]
+            cols = slice(0, count * CO)
+            out_ps = psum.tile([P, D_ROWS, PAIR * CO], F32, tag="bank")
             for i in range(D_ROWS):
                 comps = slice(i * P, (i + 1) * P)
                 nc.tensor.matmul_mx(
-                    out=out_ps[:, i, :],
+                    out=out_ps[:, i, cols],
                     lhsT=c_codes[:, comps].bitcast(FP8X4),
                     lhsT_scale=c_scales[:, comps],
-                    rhs=h_codes[:].bitcast(FP8X4),
-                    rhs_scale=h_scales[:],
+                    rhs=codes[:, cols].bitcast(FP8X4),
+                    rhs_scale=scales[:, cols],
                     start=True,
                     stop=True,
                 )
-            out_sb = out_pool.tile([P, D_ROWS, CO], F32)
-            nc.scalar.copy(out=out_sb[:], in_=out_ps[:])
+            out_sb = out_pool.tile([P, PAIR, D_ROWS, CO], F32)
+            nc.scalar.copy(
+                out=out_sb[:, :count],
+                in_=out_ps[:, :, cols].rearrange("p i (b c) -> p b i c", c=CO),
+            )
             nc.sync.dma_start(
-                out=out[b].rearrange("(p i) c -> p (i c)", i=D_ROWS),
-                in_=out_sb[:].rearrange("p i c -> p (i c)"),
+                out=out[b : b + count].rearrange("b (p i) c -> p b (i c)", i=D_ROWS),
+                in_=out_sb[:, :count].rearrange("p b i c -> p b (i c)"),
             )
 
-        for n in range(NB + AT_OUT):
-            if is_sample(n - AT_QUANTISE):
-                quantise_t2(n - AT_QUANTISE)
-            if opens_group(n - AT_QUANTISE):
-                quantise_w((n - AT_QUANTISE) // GROUP)
-            if n == ROUND_OF_C + 1:
+
+        def projections(k, a):
+            return [(project, (k, a, j, i)) for j in range(2) for i in range(D_ROWS)] if k < PAIRS else []
+
+        def w_transposes(k):
+            return [(transpose_w, (k, i, u)) for i in range(W_ROWS) for u in range(HALVES)]
+
+        def c_transposes():
+            return [(transpose_c, (i, u)) for i in range(D_ROWS) for u in range(HALVES)]
+
+        def t2_transposes(b):
+            return [
+                (transpose_t2, (b, m, j, u)) for m in range(PACK // 2) for j in range(2) for u in range(HALVES)
+            ]
+
+        def deal(plain, transposes):
+            done = 0
+            for index, (step, where) in enumerate(transposes):
+                while done < len(plain) and done * len(transposes) <= index * len(plain):
+                    plain_step, plain_where = plain[done]
+                    plain_step(*plain_where)
+                    done += 1
+                step(*where)
+
+        for a in range(PACK // 2):
+            for step, where in projections(0, a):
+                step(*where)
+
+        for n in range(PAIRS):
+            b = n * PAIR
+            if n >= 1:
+                quantise_t2(b - 1)
+            first_run = w_transposes(n) + (c_transposes() if n == 1 else []) + t2_transposes(b)
+            deal(projections(n + 1, 0), first_run)
+            if n >= 2:
+                quantise_h(b - 2 * PAIR, PAIR)
+            quantise_w(n)
+            if n == 1:
                 quantise_c()
-            if is_sample(n - AT_MULTIPLY):
-                multiply(n - AT_MULTIPLY)
-            if is_sample(n - AT_QUANTISE_H):
-                quantise_h(n - AT_QUANTISE_H)
-            if n == ROUND_OF_C:
-                transpose_c()
-            if opens_group(n - AT_TRANSPOSE):
-                transpose_w((n - AT_TRANSPOSE) // GROUP)
-            if opens_run(n - AT_TRANSPOSE):
-                for b in range(n - AT_TRANSPOSE, n - AT_TRANSPOSE + RUN):
-                    transpose_t2(b)
-            if is_sample(n - AT_PROJECT):
-                project(n - AT_PROJECT)
-            if is_sample(n - AT_T3):
-                contract_channels(n - AT_T3)
-            if is_sample(n - AT_OUT):
-                contract_ranks(n - AT_OUT)
+            if n >= 1:
+                contract_channels(b - 2)
+                contract_channels(b - 1)
+            if n >= 2:
+                contract_ranks(b - 2 * PAIR, PAIR)
+            if n >= 1:
+                multiply(b - 2)
+            quantise_t2(b)
+            if n >= 1:
+                multiply(b - 1)
+            deal(projections(n + 1, 1), t2_transposes(b + 1))
+
+        quantise_h(NB - 4, PAIR)
+        quantise_t2(NB - 1)
+        contract_channels(NB - 2)
+        contract_ranks(NB - 4, PAIR)
+        multiply(NB - 2)
+        contract_channels(NB - 1)
+        quantise_h(NB - 2, 1)
+        multiply(NB - 1)
+        contract_ranks(NB - 2, 1)
+        quantise_h(NB - 1, 1)
+        contract_ranks(NB - 1, 1)

@@ -92,6 +92,7 @@ def tile_cptensorproduct_pa_kernel(tc, x1, A, t2, w, C, out):
         w_ps = {}
         w_grouped = {}
         w_mx = {}
+        t2_sorted = {}
         t2_ps = {}
         t2_grouped = {}
         t2_mx = {}
@@ -128,11 +129,22 @@ def tile_cptensorproduct_pa_kernel(tc, x1, A, t2, w, C, out):
             )
             if (i, u) == (W_ROWS - 1, HALVES - 1):
                 grouped = work.tile([P, PAIR * CO * PACK], BF16, align_bytes=64)
-                nc.vector.tensor_copy(
+                copy = nc.scalar.copy if k % 2 else nc.vector.tensor_copy
+                copy(
                     out=grouped[:].bitcast(F32).rearrange("p (q i u) -> p q i u", i=W_ROWS, u=HALVES),
                     in_=w_ps[k][:].rearrange("p i u q -> p q i u"),
                 )
                 w_grouped[k] = grouped
+
+        def sort_t2(b):
+            if b % 4 == 0:
+                return
+            words = work.tile([P, HALVES * PACK * P], F32)
+            nc.vector.tensor_copy(
+                out=words[:].rearrange("p (u q) -> p u q", u=HALVES),
+                in_=t2_tiles[b][:].bitcast(F32).rearrange("p (q u) -> p u q", u=HALVES),
+            )
+            t2_sorted[b] = words
 
         def transpose_t2(b, m, j, u):
             if (j, u) == (0, 0):
@@ -141,11 +153,13 @@ def tile_cptensorproduct_pa_kernel(tc, x1, A, t2, w, C, out):
                 if m == 0:
                     grouped = work.tile([P, PACK * P * PACK], BF16, align_bytes=64)
                     t2_grouped[b] = grouped
-            words = t2_tiles[b][:].bitcast(F32)
-            row = (2 * m + j) * WORDS
-            nc.tensor.transpose(
-                t2_ps[b, m][:, j, u, :], words[:, row + u : row + WORDS : HALVES], ident[:]
-            )
+            if b in t2_sorted:
+                first = (u * PACK + 2 * m + j) * P
+                stationary = t2_sorted[b][:, first : first + P]
+            else:
+                row = (2 * m + j) * WORDS
+                stationary = t2_tiles[b][:].bitcast(F32)[:, row + u : row + WORDS : HALVES]
+            nc.tensor.transpose(t2_ps[b, m][:, j, u, :], stationary, ident[:])
             if (j, u) == (1, HALVES - 1):
                 out_words = t2_grouped[b][:].bitcast(F32).rearrange("p (j r u) -> p j r u", j=PACK, u=HALVES)
                 nc.scalar.copy(
@@ -264,41 +278,39 @@ def tile_cptensorproduct_pa_kernel(tc, x1, A, t2, w, C, out):
                 (transpose_t2, (b, m, j, u)) for m in range(PACK // 2) for j in range(2) for u in range(HALVES)
             ]
 
-        def deal(plain, transposes):
-            done = 0
-            for index, (step, where) in enumerate(transposes):
-                while done < len(plain) and done * len(transposes) <= index * len(plain):
-                    plain_step, plain_where = plain[done]
-                    plain_step(*plain_where)
-                    done += 1
+        def run(steps):
+            for step, where in steps:
                 step(*where)
 
         for a in range(PACK // 2):
-            for step, where in projections(0, a):
-                step(*where)
+            run(projections(0, a))
 
         for n in range(PAIRS):
             b = n * PAIR
+            sort_t2(b + 1)
             if n >= 1:
                 quantise_t2(b - 1)
-            first_run = w_transposes(n) + (c_transposes() if n == 1 else []) + t2_transposes(b)
-            deal(projections(n + 1, 0), first_run)
+            run(w_transposes(n) + (c_transposes() if n == 1 else []) + t2_transposes(b))
             if n >= 2:
                 quantise_h(b - 2 * PAIR, PAIR)
             quantise_w(n)
             if n == 1:
                 quantise_c()
+            run(projections(n + 1, 0))
             if n >= 1:
                 contract_channels(b - 2)
                 contract_channels(b - 1)
             if n >= 2:
                 contract_ranks(b - 2 * PAIR, PAIR)
+            run(projections(n + 1, 1))
             if n >= 1:
                 multiply(b - 2)
             quantise_t2(b)
+            if n + 1 < PAIRS:
+                sort_t2(b + 2)
             if n >= 1:
                 multiply(b - 1)
-            deal(projections(n + 1, 1), t2_transposes(b + 1))
+            run(t2_transposes(b + 1))
 
         quantise_h(NB - 4, PAIR)
         quantise_t2(NB - 1)

@@ -18,6 +18,8 @@ PAIR = 2
 W_ROWS = PAIR * CO // P
 PAIRS = NB // PAIR
 WORDS = CV // 2
+WARM_COLS = 512
+WARM_MATMULS = 4
 
 FLOPS = 2 * NB * R * CO * (D + CV) + 2 * NB * D * CO * R
 
@@ -77,6 +79,12 @@ def tile_cptensorproduct_pa_kernel(tc, x1, A, t2, w, C, out):
         ident = consts.tile([P, P], F32)
         make_identity(nc, ident[:])
 
+        zeros = consts.tile([P, WARM_COLS], BF16)
+        nc.vector.memset(zeros[:], 0.0)
+        warm_ps = psum.tile([P, WARM_COLS], F32, tag="bank")
+        for i in range(WARM_MATMULS):
+            nc.tensor.matmul(out=warm_ps[:], lhsT=zeros[:, :P], rhs=zeros[:], start=True, stop=True)
+
         a_chunks = consts.tile([P, D_ROWS, PACK, P], BF16)
         nc.vector.tensor_copy(
             out=a_chunks[:],
@@ -109,9 +117,11 @@ def tile_cptensorproduct_pa_kernel(tc, x1, A, t2, w, C, out):
                 if a == 0:
                     t1_sb = t1_pool.tile([P, PACK // 2, PAIR, CO, 2], F32)
                     t1_tiles[k] = t1_sb
+            chunk = 2 * a + j
+            in_place = a_in[:, i * R + chunk : (i + 1) * R : PACK]
             nc.tensor.matmul(
                 out=t1_ps[k, a][:, j],
-                lhsT=a_chunks[:, i, 2 * a + j, :],
+                lhsT=in_place if k == 0 else a_chunks[:, i, chunk, :],
                 rhs=x1_tiles[k][:, :, i * CO : (i + 1) * CO],
                 start=(i == 0),
                 stop=(i == D_ROWS - 1),
@@ -129,7 +139,7 @@ def tile_cptensorproduct_pa_kernel(tc, x1, A, t2, w, C, out):
             )
             if (i, u) == (W_ROWS - 1, HALVES - 1):
                 grouped = work.tile([P, PAIR * CO * PACK], BF16, align_bytes=64)
-                copy = nc.scalar.copy if k % 2 else nc.vector.tensor_copy
+                copy = nc.scalar.copy if k else nc.vector.tensor_copy
                 copy(
                     out=grouped[:].bitcast(F32).rearrange("p (q i u) -> p q i u", i=W_ROWS, u=HALVES),
                     in_=w_ps[k][:].rearrange("p i u q -> p q i u"),
@@ -287,12 +297,14 @@ def tile_cptensorproduct_pa_kernel(tc, x1, A, t2, w, C, out):
 
         for n in range(PAIRS):
             b = n * PAIR
-            sort_t2(b + 1)
             if n >= 1:
+                sort_t2(b + 1)
                 quantise_t2(b - 1)
             run(w_transposes(n) + (c_transposes() if n == 1 else []) + t2_transposes(b))
             if n >= 2:
                 quantise_h(b - 2 * PAIR, PAIR)
+            if n == 0:
+                sort_t2(b + 1)
             quantise_w(n)
             if n == 1:
                 quantise_c()

@@ -139,7 +139,7 @@ def tile_cptensorproduct_pa_kernel(tc, x1, A, t2, w, C, out):
             )
             if (i, u) == (W_ROWS - 1, HALVES - 1):
                 grouped = work.tile([P, PAIR * CO * PACK], BF16, align_bytes=64)
-                copy = nc.scalar.copy if k else nc.vector.tensor_copy
+                copy = nc.scalar.copy if k % 4 else nc.vector.tensor_copy
                 copy(
                     out=grouped[:].bitcast(F32).rearrange("p (q i u) -> p q i u", i=W_ROWS, u=HALVES),
                     in_=w_ps[k][:].rearrange("p i u q -> p q i u"),
@@ -147,8 +147,6 @@ def tile_cptensorproduct_pa_kernel(tc, x1, A, t2, w, C, out):
                 w_grouped[k] = grouped
 
         def sort_t2(b):
-            if b % 4 == 0:
-                return
             words = work.tile([P, HALVES * PACK * P], F32)
             nc.vector.tensor_copy(
                 out=words[:].rearrange("p (u q) -> p u q", u=HALVES),
@@ -292,46 +290,41 @@ def tile_cptensorproduct_pa_kernel(tc, x1, A, t2, w, C, out):
             for step, where in steps:
                 step(*where)
 
+        def sample(b):
+            return 0 <= b < NB
+
+        def pair_ends(b):
+            return sample(b) and b % PAIR == PAIR - 1
+
         for a in range(PACK // 2):
             run(projections(0, a))
 
-        for n in range(PAIRS):
-            b = n * PAIR
-            if n >= 1:
+        for b in range(NB + 5):
+            k, s = divmod(b, PAIR)
+            if sample(b - 3):
+                multiply(b - 3)
+            if sample(b + 1) and (b + 1) % 4:
                 sort_t2(b + 1)
+            if sample(b - 1):
                 quantise_t2(b - 1)
-            run(w_transposes(n) + (c_transposes() if n == 1 else []) + t2_transposes(b))
-            if n >= 2:
-                quantise_h(b - 2 * PAIR, PAIR)
-            if n == 0:
-                sort_t2(b + 1)
-            quantise_w(n)
-            if n == 1:
+            if b == 4:
                 quantise_c()
-            run(projections(n + 1, 0))
-            if n >= 1:
+            if sample(b):
+                run((w_transposes(k) if s == 0 else []) + t2_transposes(b))
+            if b == 3:
+                run(c_transposes())
+            if sample(b - 2):
                 contract_channels(b - 2)
-                contract_channels(b - 1)
-            if n >= 2:
-                contract_ranks(b - 2 * PAIR, PAIR)
-            run(projections(n + 1, 1))
-            if n >= 1:
-                multiply(b - 2)
-            quantise_t2(b)
-            if n + 1 < PAIRS:
-                sort_t2(b + 2)
-            if n >= 1:
-                multiply(b - 1)
-            run(t2_transposes(b + 1))
-
-        quantise_h(NB - 4, PAIR)
-        quantise_t2(NB - 1)
-        contract_channels(NB - 2)
-        contract_ranks(NB - 4, PAIR)
-        multiply(NB - 2)
-        contract_channels(NB - 1)
-        quantise_h(NB - 2, 1)
-        multiply(NB - 1)
-        contract_ranks(NB - 2, 1)
-        quantise_h(NB - 1, 1)
-        contract_ranks(NB - 1, 1)
+            if sample(b):
+                run(projections(k + 1, s))
+            if b - 3 < NB - PAIR:
+                if pair_ends(b - 3):
+                    quantise_h(b - 3 - (PAIR - 1), PAIR)
+            if sample(b) and s == 0:
+                quantise_w(k)
+            if b - 4 < NB - PAIR:
+                if pair_ends(b - 4):
+                    contract_ranks(b - 4 - (PAIR - 1), PAIR)
+            if NB - PAIR <= b - 3 < NB:
+                quantise_h(b - 3, 1)
+                contract_ranks(b - 3, 1)

@@ -18,6 +18,7 @@ PAIR = 2
 W_ROWS = PAIR * CO // P
 PAIRS = NB // PAIR
 WORDS = CV // 2
+RUN = 16
 WARM_COLS = 512
 WARM_MATMULS = 4
 
@@ -64,16 +65,19 @@ def tile_cptensorproduct_pa_kernel(tc, x1, A, t2, w, C, out):
             t2_tiles.append(t2_in)
 
         a_in = consts.tile([P, D_ROWS * R], BF16)
-        nc.sync.dma_start(out=a_in[:], in_=A.rearrange("(p i) r -> p (i r)", i=D_ROWS))
         c_in = consts.tile([P, D_ROWS * R], BF16)
         load_x1(0)
+        nc.sync.dma_start(out=a_in[:], in_=A.rearrange("(p i) r -> p (i r)", i=D_ROWS))
+        load_w(0)
+        load_t2(0)
         for k in range(PAIRS):
-            load_w(k)
-            load_t2(k * PAIR)
+            if k:
+                load_w(k)
+                load_t2(k * PAIR)
             if k + 1 < PAIRS:
                 load_x1(k + 1)
             load_t2(k * PAIR + 1)
-            if k == 0:
+            if k == 1:
                 nc.sync.dma_start(out=c_in[:], in_=C.rearrange("(p i) r -> p (i r)", i=D_ROWS))
 
         ident = consts.tile([P, P], F32)
@@ -101,6 +105,7 @@ def tile_cptensorproduct_pa_kernel(tc, x1, A, t2, w, C, out):
         w_grouped = {}
         w_mx = {}
         t2_sorted = {}
+        w_sorted = {}
         t2_ps = {}
         t2_grouped = {}
         t2_mx = {}
@@ -108,6 +113,9 @@ def tile_cptensorproduct_pa_kernel(tc, x1, A, t2, w, C, out):
         t3_tiles = {}
         h_tiles = {}
         h_mx = {}
+
+        def is_sorted(k):
+            return k % 3 != 0
 
 
         def project(k, a, j, i):
@@ -133,26 +141,34 @@ def tile_cptensorproduct_pa_kernel(tc, x1, A, t2, w, C, out):
             if (i, u) == (0, 0):
                 bank = psum.tile([P, W_ROWS, HALVES, P], F32, tag="bank")
                 w_ps[k] = bank
-            words = w_tiles[k][:].bitcast(F32)
-            nc.tensor.transpose(
-                w_ps[k][:, i, u, :], words[:, i * WORDS + u : (i + 1) * WORDS : HALVES], ident[:]
-            )
+            if is_sorted(k):
+                first = (u * W_ROWS + i) * P
+                stationary = w_sorted[k][:].bitcast(F32)[:, first : first + P]
+            else:
+                stationary = w_tiles[k][:].bitcast(F32)[:, i * WORDS + u : (i + 1) * WORDS : HALVES]
+            nc.tensor.transpose(w_ps[k][:, i, u, :], stationary, ident[:])
             if (i, u) == (W_ROWS - 1, HALVES - 1):
                 grouped = work.tile([P, PAIR * CO * PACK], BF16, align_bytes=64)
-                copy = nc.scalar.copy if k % 4 else nc.vector.tensor_copy
+                copy = nc.scalar.copy if is_sorted(k) else nc.vector.tensor_copy
                 copy(
                     out=grouped[:].bitcast(F32).rearrange("p (q i u) -> p q i u", i=W_ROWS, u=HALVES),
                     in_=w_ps[k][:].rearrange("p i u q -> p q i u"),
                 )
                 w_grouped[k] = grouped
 
-        def sort_t2(b):
-            words = work.tile([P, HALVES * PACK * P], F32)
+        def sort_rows(source, blocks):
+            words = work.tile([P, HALVES * blocks * RUN], BF16)
             nc.vector.tensor_copy(
-                out=words[:].rearrange("p (u q) -> p u q", u=HALVES),
-                in_=t2_tiles[b][:].bitcast(F32).rearrange("p (q u) -> p u q", u=HALVES),
+                out=words[:].rearrange("p (u g e) -> p u g e", u=HALVES, e=RUN),
+                in_=source[:].rearrange("p (g u e) -> p u g e", u=HALVES, e=RUN),
             )
-            t2_sorted[b] = words
+            return words
+
+        def sort_t2(b):
+            t2_sorted[b] = sort_rows(t2_tiles[b], PACK * CV // (HALVES * RUN))
+
+        def sort_w(k):
+            w_sorted[k] = sort_rows(w_tiles[k], W_ROWS * CV // (HALVES * RUN))
 
         def transpose_t2(b, m, j, u):
             if (j, u) == (0, 0):
@@ -161,9 +177,9 @@ def tile_cptensorproduct_pa_kernel(tc, x1, A, t2, w, C, out):
                 if m == 0:
                     grouped = work.tile([P, PACK * P * PACK], BF16, align_bytes=64)
                     t2_grouped[b] = grouped
-            if b in t2_sorted:
+            if is_sorted(b // PAIR):
                 first = (u * PACK + 2 * m + j) * P
-                stationary = t2_sorted[b][:, first : first + P]
+                stationary = t2_sorted[b][:].bitcast(F32)[:, first : first + P]
             else:
                 row = (2 * m + j) * WORDS
                 stationary = t2_tiles[b][:].bitcast(F32)[:, row + u : row + WORDS : HALVES]
@@ -303,7 +319,9 @@ def tile_cptensorproduct_pa_kernel(tc, x1, A, t2, w, C, out):
             k, s = divmod(b, PAIR)
             if sample(b - 3):
                 multiply(b - 3)
-            if sample(b + 1) and (b + 1) % 4:
+            if sample(b + 1) and is_sorted((b + 1) // PAIR):
+                if s == 1:
+                    sort_w(k + 1)
                 sort_t2(b + 1)
             if sample(b - 1):
                 quantise_t2(b - 1)

@@ -68,15 +68,12 @@ def tile_cptensorproduct_pa_kernel(tc, x1, A, t2, w, C, out):
         c_in = consts.tile([P, D_ROWS * R], BF16)
         load_x1(0)
         nc.sync.dma_start(out=a_in[:], in_=A.rearrange("(p i) r -> p (i r)", i=D_ROWS))
-        load_w(0)
-        load_t2(0)
         for k in range(PAIRS):
+            load_w(k)
+            for b in range(k * PAIR, (k + 1) * PAIR):
+                load_t2(b)
             if k:
-                load_w(k)
-                load_t2(k * PAIR)
-            if k + 1 < PAIRS:
-                load_x1(k + 1)
-            load_t2(k * PAIR + 1)
+                load_x1(k)
             if k == 1:
                 nc.sync.dma_start(out=c_in[:], in_=C.rearrange("(p i) r -> p (i r)", i=D_ROWS))
 
@@ -84,7 +81,7 @@ def tile_cptensorproduct_pa_kernel(tc, x1, A, t2, w, C, out):
         make_identity(nc, ident[:])
 
         zeros = consts.tile([P, WARM_COLS], BF16)
-        nc.vector.memset(zeros[:], 0.0)
+        nc.vector.memset(zeros[:].bitcast(U32), 0)
         warm_ps = psum.tile([P, WARM_COLS], F32, tag="bank")
         for i in range(WARM_MATMULS):
             nc.tensor.matmul(out=warm_ps[:], lhsT=zeros[:, :P], rhs=zeros[:], start=True, stop=True)
@@ -289,7 +286,7 @@ def tile_cptensorproduct_pa_kernel(tc, x1, A, t2, w, C, out):
 
 
         def projections(k, a):
-            return [(project, (k, a, j, i)) for j in range(2) for i in range(D_ROWS)] if k < PAIRS else []
+            return [(project, (k, a, j, i)) for j in range(2) for i in range(D_ROWS)]
 
         def w_transposes(k):
             return [(transpose_w, (k, i, u)) for i in range(W_ROWS) for u in range(HALVES)]
@@ -333,8 +330,8 @@ def tile_cptensorproduct_pa_kernel(tc, x1, A, t2, w, C, out):
                 run(c_transposes())
             if sample(b - 2):
                 contract_channels(b - 2)
-            if sample(b):
-                run(projections(k + 1, s))
+            if sample(b) and k:
+                run(projections(k, s))
             if b - 3 < NB - PAIR:
                 if pair_ends(b - 3):
                     quantise_h(b - 3 - (PAIR - 1), PAIR)

from contextlib import ExitStack

import concourse.mybir as mybir
from concourse.masks import make_identity

F32 = mybir.dt.float32
BF16 = mybir.dt.bfloat16
U32 = mybir.dt.uint32
U8 = mybir.dt.uint8
FP8X4 = mybir.dt.float8_e4m3fn_x4

NB, D, CO, CV, R = 16, 256, 128, 512, 512
P = 128
PACK = 4
HALVES = 2
D_ROWS = D // P
PAIR = 2
W_ROWS = PAIR * CO // P
PAIRS = NB // PAIR
WORDS = CV // 2
RUN = 16
WARM_COLS = 512
WARM_MATMULS = 4

FLOPS = 2 * NB * R * CO * (D + CV) + 2 * NB * D * CO * R


def tile_cptensorproduct_pa_kernel(tc, x1, A, t2, w, C, out):
    nc = tc.nc
    with ExitStack() as ctx:
        consts = ctx.enter_context(tc.tile_pool(name="consts", bufs=1))
        loads = ctx.enter_context(tc.tile_pool(name="loads", bufs=PAIRS))
        t2_pool = ctx.enter_context(tc.tile_pool(name="t2_pool", bufs=NB))
        work = ctx.enter_context(tc.tile_pool(name="work", bufs=4))
        t1_pool = ctx.enter_context(tc.tile_pool(name="t1_pool", bufs=5))
        out_pool = ctx.enter_context(tc.tile_pool(name="out_pool", bufs=PAIRS + 1))
        psum = ctx.enter_context(tc.psum_pool(name="psum", bufs=8))

        ctx.enter_context(tc.manual_schedule())

        x1_tiles = []
        w_tiles = []
        t2_tiles = []
        w_rows = w.rearrange("b o v -> (b o) v")

        def load_x1(k):
            x1_in = loads.tile([P, PAIR, D_ROWS * CO], BF16)
            nc.sync.dma_start(
                out=x1_in[:],
                in_=x1[k * PAIR : (k + 1) * PAIR].rearrange("b (p i) c -> p b (i c)", i=D_ROWS),
            )
            x1_tiles.append(x1_in)

        def load_w(k):
            w_in = loads.tile([P, W_ROWS * CV], BF16)
            nc.sync.dma_start(
                out=w_in[:],
                in_=w_rows[k * PAIR * CO : (k + 1) * PAIR * CO].rearrange("(p i) v -> p (i v)", i=W_ROWS),
            )
            w_tiles.append(w_in)

        def load_t2(b):
            t2_in = t2_pool.tile([P, PACK * CV], BF16)
            nc.sync.dma_start(out=t2_in[:], in_=t2[b].rearrange("(p j) v -> p (j v)", j=PACK))
            t2_tiles.append(t2_in)

        a_in = consts.tile([P, D_ROWS * R], BF16)
        c_in = consts.tile([P, D_ROWS * R], BF16)
        load_x1(0)
        nc.sync.dma_start(out=a_in[:], in_=A.rearrange("(p i) r -> p (i r)", i=D_ROWS))
        for k in range(PAIRS):
            load_w(k)
            for b in range(k * PAIR, (k + 1) * PAIR):
                load_t2(b)
            if k:
                load_x1(k)
            if k == 1:
                nc.sync.dma_start(out=c_in[:], in_=C.rearrange("(p i) r -> p (i r)", i=D_ROWS))

        ident = consts.tile([P, P], F32)
        make_identity(nc, ident[:])

        zeros = consts.tile([P, WARM_COLS], BF16)
        nc.vector.memset(zeros[:].bitcast(U32), 0)
        warm_ps = psum.tile([P, WARM_COLS], F32, tag="bank")
        for i in range(WARM_MATMULS):
            nc.tensor.matmul(out=warm_ps[:], lhsT=zeros[:, :P], rhs=zeros[:], start=True, stop=True)

        a_chunks = consts.tile([P, D_ROWS, PACK, P], BF16)
        nc.vector.tensor_copy(
            out=a_chunks[:],
            in_=a_in[:].rearrange("p (i m j) -> p i j m", i=D_ROWS, j=PACK),
        )

        c_grouped = consts.tile([P, D_ROWS * P * PACK], BF16, align_bytes=64)
        c_codes = consts.tile([P, D_ROWS * P], U32, align_bytes=64)
        c_scales = consts.tile([P, D_ROWS * P], U8, align_bytes=64)

        t1_ps = {}
        t1_tiles = {}
        w_ps = {}
        w_grouped = {}
        w_mx = {}
        t2_sorted = {}
        w_sorted = {}
        t2_ps = {}
        t2_grouped = {}
        t2_mx = {}
        c_ps = {}
        t3_tiles = {}
        h_tiles = {}
        h_mx = {}

        def is_sorted(k):
            return k % 3 != 0


        def project(k, a, j, i):
            if (j, i) == (0, 0):
                bank = psum.tile([P, 2, PAIR, CO], F32, tag="bank")
                t1_ps[k, a] = bank
                if a == 0:
                    t1_sb = t1_pool.tile([P, PACK // 2, PAIR, CO, 2], F32)
                    t1_tiles[k] = t1_sb
            chunk = 2 * a + j
            in_place = a_in[:, i * R + chunk : (i + 1) * R : PACK]
            nc.tensor.matmul(
                out=t1_ps[k, a][:, j],
                lhsT=in_place if k == 0 else a_chunks[:, i, chunk, :],
                rhs=x1_tiles[k][:, :, i * CO : (i + 1) * CO],
                start=(i == 0),
                stop=(i == D_ROWS - 1),
            )
            if (j, i) == (1, D_ROWS - 1):
                nc.scalar.copy(out=t1_tiles[k][:, a], in_=t1_ps[k, a][:].rearrange("p j b c -> p b c j"))

        def transpose_w(k, i, u):
            if (i, u) == (0, 0):
                bank = psum.tile([P, W_ROWS, HALVES, P], F32, tag="bank")
                w_ps[k] = bank
            if is_sorted(k):
                first = (u * W_ROWS + i) * P
                stationary = w_sorted[k][:].bitcast(F32)[:, first : first + P]
            else:
                stationary = w_tiles[k][:].bitcast(F32)[:, i * WORDS + u : (i + 1) * WORDS : HALVES]
            nc.tensor.transpose(w_ps[k][:, i, u, :], stationary, ident[:])
            if (i, u) == (W_ROWS - 1, HALVES - 1):
                grouped = work.tile([P, PAIR * CO * PACK], BF16, align_bytes=64)
                copy = nc.scalar.copy if is_sorted(k) else nc.vector.tensor_copy
                copy(
                    out=grouped[:].bitcast(F32).rearrange("p (q i u) -> p q i u", i=W_ROWS, u=HALVES),
                    in_=w_ps[k][:].rearrange("p i u q -> p q i u"),
                )
                w_grouped[k] = grouped

        def sort_rows(source, blocks):
            words = work.tile([P, HALVES * blocks * RUN], BF16)
            nc.vector.tensor_copy(
                out=words[:].rearrange("p (u g e) -> p u g e", u=HALVES, e=RUN),
                in_=source[:].rearrange("p (g u e) -> p u g e", u=HALVES, e=RUN),
            )
            return words

        def sort_t2(b):
            t2_sorted[b] = sort_rows(t2_tiles[b], PACK * CV // (HALVES * RUN))

        def sort_w(k):
            w_sorted[k] = sort_rows(w_tiles[k], W_ROWS * CV // (HALVES * RUN))

        def transpose_t2(b, m, j, u):
            if (j, u) == (0, 0):
                bank = psum.tile([P, 2, HALVES, P], F32, tag="bank")
                t2_ps[b, m] = bank
                if m == 0:
                    grouped = work.tile([P, PACK * P * PACK], BF16, align_bytes=64)
                    t2_grouped[b] = grouped
            if is_sorted(b // PAIR):
                first = (u * PACK + 2 * m + j) * P
                stationary = t2_sorted[b][:].bitcast(F32)[:, first : first + P]
            else:
                row = (2 * m + j) * WORDS
                stationary = t2_tiles[b][:].bitcast(F32)[:, row + u : row + WORDS : HALVES]
            nc.tensor.transpose(t2_ps[b, m][:, j, u, :], stationary, ident[:])
            if (j, u) == (1, HALVES - 1):
                out_words = t2_grouped[b][:].bitcast(F32).rearrange("p (j r u) -> p j r u", j=PACK, u=HALVES)
                nc.scalar.copy(
                    out=out_words[:, 2 * m : 2 * m + 2],
                    in_=t2_ps[b, m][:].rearrange("p j u r -> p j r u"),
                )

        def transpose_c(i, u):
            if (i, u) == (0, 0):
                bank = psum.tile([P, D_ROWS, HALVES, P], F32, tag="bank")
                c_ps[0] = bank
            words = c_in[:].bitcast(F32)
            nc.tensor.transpose(
                c_ps[0][:, i, u, :], words[:, i * (R // 2) + u : (i + 1) * (R // 2) : HALVES], ident[:]
            )
            if (i, u) == (D_ROWS - 1, HALVES - 1):
                nc.vector.tensor_copy(
                    out=c_grouped[:].bitcast(F32).rearrange("p (i d u) -> p i d u", i=D_ROWS, u=HALVES),
                    in_=c_ps[0][:].rearrange("p i u d -> p i d u"),
                )


        def quantise_w(k):
            codes = work.tile([P, PAIR * CO], U32, align_bytes=64)
            scales = work.tile([P, PAIR * CO], U8, align_bytes=64)
            nc.vector.quantize_mx(out=codes[:].bitcast(FP8X4), scales=scales[:], in_=w_grouped[k][:])
            w_mx[k] = (codes, scales)

        def quantise_t2(b):
            codes = work.tile([P, PACK * P], U32, align_bytes=64)
            scales = work.tile([P, PACK * P], U8, align_bytes=64)
            nc.vector.quantize_mx(out=codes[:].bitcast(FP8X4), scales=scales[:], in_=t2_grouped[b][:])
            t2_mx[b] = (codes, scales)

        def quantise_c():
            nc.vector.quantize_mx(out=c_codes[:].bitcast(FP8X4), scales=c_scales[:], in_=c_grouped[:])

        def contract_channels(b):
            t2_codes, t2_scales = t2_mx[b]
            w_codes, w_scales = w_mx[b // PAIR]
            w_cols = slice((b % PAIR) * CO, (b % PAIR + 1) * CO)
            t3_ps = psum.tile([P, PACK, CO], F32, tag="bank")
            for j in range(PACK):
                ranks = slice(j * P, (j + 1) * P)
                nc.tensor.matmul_mx(
                    out=t3_ps[:, j, :],
                    lhsT=t2_codes[:, ranks].bitcast(FP8X4),
                    lhsT_scale=t2_scales[:, ranks],
                    rhs=w_codes[:, w_cols].bitcast(FP8X4),
                    rhs_scale=w_scales[:, w_cols],
                    start=True,
                    stop=True,
                )
            t3_tiles[b] = t3_ps

        def multiply(b):
            k, s = divmod(b, PAIR)
            if s == 0:
                h_pair = work.tile([P, PAIR, CO, PACK], BF16, align_bytes=64)
                h_tiles[k] = h_pair
            nc.vector.tensor_tensor(
                out=h_tiles[k][:, s].rearrange("p c (a j) -> p c a j", a=PACK // 2),
                in0=t1_tiles[k][:, :, s].rearrange("p a c j -> p c a j"),
                in1=t3_tiles[b][:].rearrange("p (a j) c -> p c a j", a=PACK // 2),
                op=mybir.AluOpType.mult,
            )

        def quantise_h(b, count):
            k, s = divmod(b, PAIR)
            codes = work.tile([P, PAIR * CO], U32, align_bytes=64)
            scales = work.tile([P, PAIR * CO], U8, align_bytes=64)
            nc.vector.quantize_mx(
                out=codes[:, : count * CO].bitcast(FP8X4),
                scales=scales[:, : count * CO],
                in_=h_tiles[k][:, s : s + count].rearrange("p b c t -> p (b c t)"),
            )
            h_mx[b] = (codes, scales)

        def contract_ranks(b, count):
            codes, scales = h_mx[b]
            cols = slice(0, count * CO)
            out_ps = psum.tile([P, D_ROWS, PAIR * CO], F32, tag="bank")
            for i in range(D_ROWS):
                comps = slice(i * P, (i + 1) * P)
                nc.tensor.matmul_mx(
                    out=out_ps[:, i, cols],
                    lhsT=c_codes[:, comps].bitcast(FP8X4),
                    lhsT_scale=c_scales[:, comps],
                    rhs=codes[:, cols].bitcast(FP8X4),
                    rhs_scale=scales[:, cols],
                    start=True,
                    stop=True,
                )
            out_sb = out_pool.tile([P, PAIR, D_ROWS, CO], F32)
            nc.scalar.copy(
                out=out_sb[:, :count],
                in_=out_ps[:, :, cols].rearrange("p i (b c) -> p b i c", c=CO),
            )
            nc.sync.dma_start(
                out=out[b : b + count].rearrange("b (p i) c -> p b (i c)", i=D_ROWS),
                in_=out_sb[:, :count].rearrange("p b i c -> p b (i c)"),
            )


        def projections(k, a):
            return [(project, (k, a, j, i)) for j in range(2) for i in range(D_ROWS)]

        def w_transposes(k):
            return [(transpose_w, (k, i, u)) for i in range(W_ROWS) for u in range(HALVES)]

        def c_transposes():
            return [(transpose_c, (i, u)) for i in range(D_ROWS) for u in range(HALVES)]

        def t2_transposes(b):
            return [
                (transpose_t2, (b, m, j, u)) for m in range(PACK // 2) for j in range(2) for u in range(HALVES)
            ]

        def run(steps):
            for step, where in steps:
                step(*where)

        def sample(b):
            return 0 <= b < NB

        def pair_ends(b):
            return sample(b) and b % PAIR == PAIR - 1

        for a in range(PACK // 2):
            run(projections(0, a))

        for b in range(NB + 5):
            k, s = divmod(b, PAIR)
            if sample(b - 3):
                multiply(b - 3)
            if sample(b + 1) and is_sorted((b + 1) // PAIR):
                if s == 1:
                    sort_w(k + 1)
                sort_t2(b + 1)
            if sample(b - 1):
                quantise_t2(b - 1)
            if b == 4:
                quantise_c()
            if sample(b):
                run((w_transposes(k) if s == 0 else []) + t2_transposes(b))
            if b == 3:
                run(c_transposes())
            if sample(b - 2):
                contract_channels(b - 2)
            if sample(b) and k:
                run(projections(k, s))
            if b - 3 < NB - PAIR:
                if pair_ends(b - 3):
                    quantise_h(b - 3 - (PAIR - 1), PAIR)
            if sample(b) and s == 0:
                quantise_w(k)
            if b - 4 < NB - PAIR:
                if pair_ends(b - 4):
                    contract_ranks(b - 4 - (PAIR - 1), PAIR)
            if NB - PAIR <= b - 3 < NB:
                quantise_h(b - 3, 1)
                contract_ranks(b - 3, 1)
